import numpy as np
import ml_dtypes


def mxq(x, axis, fmt="e4m3"):
    dtype, down = {"e4m3": (ml_dtypes.float8_e4m3fn, 7), "e5m2": (ml_dtypes.float8_e5m2, 14)}[fmt]
    v = np.moveaxis(np.asarray(x, np.float32).astype(ml_dtypes.bfloat16).astype(np.float64), axis, -1)
    blocks = v.reshape(v.shape[:-1] + (-1, 32))
    amax = np.abs(blocks).max(-1, keepdims=True)
    byte = np.maximum(np.where(amax > 0, np.frexp(amax)[1] - 1 + 127, 0) - down, 1)
    scale = np.exp2(byte - 127.0)
    codes = (blocks / scale).astype(np.float32).astype(dtype).astype(np.float64)
    return np.moveaxis((codes * scale).reshape(v.shape), -1, axis)


WIDE = False


def mx_kscale(k):
    if not WIDE:
        return np.ones(k)
    levels = np.array([18, -18])
    if k % 512:
        return np.exp2(np.random.permutation(np.resize(levels, k // 32))).repeat(32)
    a = np.empty((k // 512, 16))
    for p in range(k // 512):
        a[p, :8] = np.random.permutation(np.resize(levels, 8))
        for g in range(8):
            far = levels[np.abs(levels - a[p, g]) >= 10]
            a[p, g + 8] = far[np.random.randint(len(far))]
    return np.exp2(a.ravel()).repeat(32)


BF16 = ml_dtypes.bfloat16


def bf(x):
    return np.asarray(x, np.float32).astype(BF16)


def f64(x):
    return np.asarray(x).astype(np.float64)


B, N, D, F1, F2, F3, G1, G2 = 64, 8, 512, 512, 512, 1024, 512, 512
ALPHA = 0.2


def lrelu(v):
    return np.maximum(v, ALPHA * v)


def dlrelu(v):
    return np.where(v > 0, 1.0, ALPHA)


def setup_inputs():
    s = mx_kscale(B * N * N).reshape(B, N, N)[:, :, :1]
    u = mx_kscale(G1)
    v = mx_kscale(F3)
    vx = np.concatenate([v, np.ones(D)])
    e2_0 = bf(lrelu(np.random.standard_normal((B, N, N, F2))))
    x = bf(np.random.standard_normal((B, N, D)))
    fe_w2_0 = bf(np.random.standard_normal((F2, F3)) * (12.0 / N) / np.sqrt(F2))
    fe_b2 = bf(np.random.standard_normal(F3) * (3.0 / N))
    fn_w0_0 = bf(np.random.standard_normal((F3 + D, G1)) * 0.25 / np.sqrt(F3 + D))
    fn_b0 = bf(np.random.standard_normal(G1) * 0.3)
    g = bf(np.random.standard_normal((B, N, G1)) * np.exp2(np.random.randint(-6, 1, (B, N, 1))) * 8.0 / s * u)
    z1 = (f64(e2_0).reshape(B * N * N, F2) @ f64(fe_w2_0)).reshape(B, N, N, F3) + f64(fe_b2)
    h = np.concatenate([lrelu(z1).sum(axis=2), f64(x)], axis=-1)
    z2 = h @ f64(fn_w0_0) + f64(fn_b0)
    return {"e2": bf(f64(e2_0) * s[..., None]),
            "x": x,
            "fe_w2": bf(f64(fe_w2_0) / v),
            "fe_b2": fe_b2,
            "fn_w0": bf(f64(fn_w0_0) * vx[:, None] / u),
            "fn_b0": fn_b0,
            "z1": np.asarray(z1, np.float32),
            "z2": np.asarray(z2, np.float32),
            "grad_out": g}


def reference(e2, x, fe_w2, fe_b2, fn_w0, fn_b0, z1, z2, grad_out):
    dz2 = (f64(grad_out) * dlrelu(f64(z2))).reshape(B * N, G1)
    wa = f64(fn_w0)[:F3]
    dagg = mxq(dz2, 1, "e5m2") @ mxq(wa, 1, "e4m3").T
    dz1 = (dagg.reshape(B, N, 1, F3) * dlrelu(f64(z1))).reshape(B * N * N, F3)
    de2 = mxq(dz1, 1, "e5m2") @ mxq(f64(fe_w2), 1, "e4m3").T
    ef = f64(e2).reshape(B * N * N, F2)
    dw = mxq(ef, 0, "e4m3").T @ mxq(dz1, 0, "e5m2")
    return de2.reshape(B, N, N, F2), dw

@@ -1,0 +1,338 @@
+from contextlib import ExitStack
+
+import concourse.mybir as mybir
+from concourse.masks import make_identity
+
+F32 = mybir.dt.float32
+BF16 = mybir.dt.bfloat16
+U32 = mybir.dt.uint32
+U8 = mybir.dt.uint8
+E4M3 = mybir.dt.float8_e4m3fn_x4
+E5M2 = mybir.dt.float8_e5m2_x4
+ALU = mybir.AluOpType
+
+FLOPS = 2 * 512 * 512 * 1024 + 2 * 2 * 4096 * 512 * 1024
+BYTES = 2 * (4096 * 512 + 2 * 512 * 1024 + 512 * 512) + 4 * (4096 * 1024 + 512 * 512 + 4096 * 512 + 512 * 1024)
+
+P = 128
+GROUPS = 8
+HALVES = 16
+SLOPE = 0.2
+SPLIT = 5
+
+
+def tile_graph_gan_pb_v_kernel(tc, e2, x, fe_w2, fe_b2, fn_w0, fn_b0, z1, z2, grad_out, out_0, out_1):
+    nc = tc.nc
+    with ExitStack() as ctx:
+        sb = ctx.enter_context(tc.tile_pool(name="sb", bufs=1))
+        ps = ctx.enter_context(tc.psum_pool(name="ps", bufs=1))
+        ctx.enter_context(tc.manual_schedule())
+
+        def st(shape, dtype, name, tag, bufs):
+            return sb.tile(shape, dtype, name=name, tag=tag, bufs=bufs, align_bytes=64)
+
+        def pt(tag, bufs):
+            t = ps.tile([P, 512], F32, name=tag, tag=tag, bufs=bufs)
+            return t
+
+        z1v = z1.flatten_outer_dims().rearrange("(i p j) w -> i p j w", p=P, j=4)
+        e2v = e2.flatten_outer_dims().rearrange("(i p j) f -> i p j f", p=P, j=4)
+        o0v = out_0.flatten_outer_dims().rearrange("(i p j) f -> i p j f", p=P, j=4)
+        wav = fn_w0[0:1024, :].rearrange("(g m t) k -> g m t k", g=2, t=4)
+        fev = fe_w2.rearrange("(r p) k -> p r k", p=P)
+        z2v = z2.flatten_outer_dims().rearrange("(n p) k -> p n k", p=P)
+        gov = grad_out.flatten_outer_dims().rearrange("(n p) k -> p n k", p=P)
+
+        ident = st([P, P], F32, "ident", "ident", 1)
+        make_identity(nc, ident[:])
+
+        z2t = st([P, 4, 512], F32, "z2t", "io8", 3)
+        got = st([P, 4, 512], BF16, "got", "dz", 3)
+        nc.sync.dma_start(out=z2t[:, 0, :], in_=z2v[:, 0, :])
+        nc.sync.dma_start(out=got[:, 0, :], in_=gov[:, 0, :])
+        wa_raw = st([P, 2, 4, 512], BF16, "wa_raw", "io8", 3)
+        nc.sync.dma_start(out=wa_raw[:, 0], in_=wav[0])
+
+        z1t = {}
+        e2t = {}
+
+        def load_z1(s):
+            z1t[s] = st([P, 4, 512], F32, "z1t", "z1t", 5)
+            g = s % 2
+            nc.sync.dma_start(out=z1t[s][:], in_=z1v[s // 2][:, :, 512 * g:512 * (g + 1)])
+
+        def load_e2(i):
+            e2t[i] = st([P, 4, 512], BF16, "e2t", "e2t", 2)
+            nc.sync.dma_start(out=e2t[i][:], in_=e2v[i])
+
+        load_z1(0)
+        nc.sync.dma_start(out=wa_raw[:, 1], in_=wav[1])
+        load_z1(1)
+        nc.sync.dma_start(out=z2t[:, 1:4, :], in_=z2v[:, 1:4, :])
+        nc.sync.dma_start(out=got[:, 1:4, :], in_=gov[:, 1:4, :])
+        load_e2(0)
+        load_z1(2)
+        fe_raw = st([P, 4, 1024], BF16, "fe_raw", "io8", 3)
+        nc.sync.dma_start(out=fe_raw[:], in_=fev)
+        load_z1(3)
+        load_e2(1)
+        load_z1(4)
+
+        dz2 = st([P, 4, 512], BF16, "dz2", "dz", 3)
+        dz2_t = st([P, 4096], BF16, "dz2_t", "turned", 1)
+        dz2_c = st([P, 1024], U32, "dz2_c", "dz2_c", 1)
+        dz2_s = st([P, 1024], U8, "dz2_s", "dz2_s", 1)
+
+        def dz2_values(a, b):
+            nc.vector.tensor_scalar(out=z2t[:, a:b, :], in0=z2t[:, a:b, :], scalar1=0.0, scalar2=SLOPE, op0=ALU.is_gt, op1=ALU.max)
+            nc.vector.tensor_tensor(out=dz2[:, a:b, :], in0=got[:, a:b, :], in1=z2t[:, a:b, :], op=ALU.mult)
+
+        def dz2_turn(n):
+            tp = pt("tp", 3)
+            words = dz2[:, n, :].bitcast(F32)
+            for u in range(2):
+                nc.tensor.transpose(tp[:, P * u:P * (u + 1)], words[:, u:256:2], ident[:])
+            return tp
+
+        def dz2_copy(n, tp):
+            dst = dz2_t[:].bitcast(F32)[:, 512 * n:512 * (n + 1)].rearrange("p (n d u) -> p n d u", d=2, u=2)
+            src = tp[:, 0:256].rearrange("p (u n) -> p n u", u=2).unsqueeze(2).to_broadcast([P, P, 2, 2])
+            nc.vector.tensor_copy(out=dst, in_=src)
+
+        def dz2_quant(a, b):
+            nc.vector.quantize_mx(out=dz2_c[:, 256 * a:256 * b].bitcast(E5M2), scales=dz2_s[:, 256 * a:256 * b], in_=dz2_t[:, 1024 * a:1024 * b])
+
+        def turn_words(words, bank_cols, tp):
+            for k, (row, lo) in enumerate(bank_cols):
+                nc.tensor.transpose(tp[:, P * k:P * (k + 1)], words[row][:, lo:lo + 255:2], ident[:])
+
+        def copy_words(eng_copy, dst_words, tp):
+            eng_copy(out=dst_words.rearrange("p (s m u) -> p s m u", s=2, u=2), in_=tp[:].rearrange("p (s u m) -> p s m u", s=2, u=2))
+
+        wa_g = st([P, 4096], BF16, "wa_g", "mk", 3)
+        wa_c = st([P, 1024], U32, "wa_c", "wa_c", 1)
+        wa_s = st([P, 1024], U8, "wa_s", "wa_s", 1)
+
+        def wa_turn(g, b):
+            tp = pt("tp", 3)
+            words = [wa_raw[:, g, t, :].bitcast(F32) for t in range(4)]
+            turn_words(words, [(2 * b + s, u) for s in range(2) for u in range(2)], tp)
+            return tp
+
+        def wa_copy(eng_copy, g, b, tp):
+            c0 = 1024 * g + 512 * b
+            copy_words(eng_copy, wa_g[:].bitcast(F32)[:, c0:c0 + 512], tp)
+
+        def wa_quant(g):
+            nc.vector.quantize_mx(out=wa_c[:, 512 * g:512 * (g + 1)].bitcast(E4M3), scales=wa_s[:, 512 * g:512 * (g + 1)], in_=wa_g[:, 2048 * g:2048 * (g + 1)])
+
+        d_ps = {}
+        mk = {}
+        dz = {}
+        dzc = {}
+        dzs = {}
+        dzt = {}
+        dtc = {}
+        dts = {}
+        tps = {}
+
+        def dagg(s):
+            i, g = s // 2, s % 2
+            d_ps[s] = pt("d", 2)
+            nc.tensor.matmul_mx(out=d_ps[s][:], lhsT=dz2_c[:, P * i:P * (i + 1)].bitcast(E5M2), lhsT_scale=dz2_s[:, P * i:P * (i + 1)],
+                                rhs=wa_c[:, 512 * g:512 * (g + 1)].bitcast(E4M3), rhs_scale=wa_s[:, 512 * g:512 * (g + 1)], start=True, stop=True)
+
+        def mask(s):
+            mk[s] = st([P, 4, 512], F32, "mk", "mk", 3)
+            nc.vector.tensor_scalar(out=mk[s][:].rearrange("p j (t q) -> p j q t", t=4), in0=z1t[s][:].rearrange("p j (q t) -> p j q t", t=4),
+                                    scalar1=0.0, scalar2=SLOPE, op0=ALU.is_gt, op1=ALU.max)
+
+        def product(s):
+            dz[s] = st([P, 2048], BF16, "dz", "dz", 3)
+            nc.vector.tensor_tensor(out=dz[s][:].rearrange("p (c i j) -> p c j i", i=2, j=4), in0=mk[s][:].rearrange("p j (c i) -> p c j i", i=2),
+                                    in1=d_ps[s][:].rearrange("p (c i) -> p c i", i=2).unsqueeze(2).to_broadcast([P, 256, 4, 2]), op=ALU.mult)
+
+        def quant_edges(s):
+            dzc[s] = st([P, 512], U32, "dzc", "dzc", HALVES)
+            dzs[s] = st([P, 512], U8, "dzs", "dzs", HALVES)
+            nc.vector.quantize_mx(out=dzc[s][:].bitcast(E5M2), scales=dzs[s][:], in_=dz[s][:])
+
+        def turn(s):
+            words = dz[s][:].bitcast(F32)
+            tps[s] = []
+            for h in range(2):
+                tp = pt("tp", 3)
+                for t in range(4):
+                    nc.tensor.transpose(tp[:, P * t:P * (t + 1)], words[:, 256 * t + h:256 * (t + 1):2], ident[:])
+                tps[s].append(tp)
+
+        def untangle(eng_copy, s, h):
+            if h == 0:
+                dzt[s] = st([P, 2048], BF16, "dzt", "dzt", 3)
+            eng_copy(out=dzt[s][:, 1024 * h:1024 * (h + 1)].rearrange("p (e n t) -> p e n t", e=2, t=4),
+                     in_=tps[s][h][:].bitcast(BF16).rearrange("p (t n e) -> p e n t", t=4, e=2))
+
+        def quant_feats(s):
+            dtc[s] = st([P, 512], U32, "dtc", "dtc", 4)
+            dts[s] = st([P, 512], U8, "dts", "dts", 4)
+            nc.vector.quantize_mx(out=dtc[s][:].bitcast(E5M2), scales=dts[s][:], in_=dzt[s][:])
+
+        eg = {}
+        ec = {}
+        es = {}
+
+        def e2_copy(i, h):
+            if h == 0:
+                eg[i] = st([P, 2048], BF16, "eg", "eg", 2)
+            nc.scalar.copy(out=eg[i][:, 1024 * h:1024 * (h + 1)].rearrange("p (c i j) -> p c j i", i=4, j=4),
+                           in_=e2t[i][:, :, 256 * h:256 * (h + 1)].rearrange("p j (c i) -> p c j i", i=4))
+
+        def e2_quant(i):
+            ec[i] = st([P, 512], U32, "ec", "ec", GROUPS)
+            es[i] = st([P, 512], U8, "es", "es", GROUPS)
+            nc.vector.quantize_mx(out=ec[i][:].bitcast(E4M3), scales=es[i][:], in_=eg[i][:])
+
+        fe_gs = []
+        fe_c = st([P, 1024], U32, "fe_c", "fe_c", 1)
+        fe_s = st([P, 1024], U8, "fe_s", "fe_s", 1)
+
+        def fe_turn(g, b):
+            if not fe_gs:
+                fe_gs.append(st([P, 4096], BF16, "fe_g", "turned", 1))
+            tp = pt("tp", 3)
+            words = [fe_raw[:, r, :].bitcast(F32) for r in range(4)]
+            turn_words(words, [(2 * b + r, 256 * g + u) for r in range(2) for u in range(2)], tp)
+            return tp
+
+        def fe_copy(eng_copy, g, b, tp):
+            c0 = 1024 * g + 512 * b
+            copy_words(eng_copy, fe_gs[0][:].bitcast(F32)[:, c0:c0 + 512], tp)
+
+        def fe_quant(g):
+            nc.vector.quantize_mx(out=fe_c[:, 512 * g:512 * (g + 1)].bitcast(E4M3), scales=fe_s[:, 512 * g:512 * (g + 1)], in_=fe_gs[0][:, 2048 * g:2048 * (g + 1)])
+
+        mms = {}
+        outs = {}
+
+        def de2(i, j):
+            mms[i, j] = pt("mm", 3)
+            for g in range(2):
+                s = 2 * i + g
+                nc.tensor.matmul_mx(out=mms[i, j][:], lhsT=dtc[s][:, P * j:P * (j + 1)].bitcast(E5M2), lhsT_scale=dts[s][:, P * j:P * (j + 1)],
+                                    rhs=fe_c[:, 512 * g:512 * (g + 1)].bitcast(E4M3), rhs_scale=fe_s[:, 512 * g:512 * (g + 1)], start=(g == 0), stop=(g == 1))
+
+        def de2_copy(eng_copy, i, j):
+            if j == 0:
+                outs[i] = st([P, 4, 512], F32, "o", "io8", 3)
+            eng_copy(out=outs[i][:, j, :], in_=mms[i, j][:])
+
+        def store(i, a, b):
+            nc.sync.dma_start(out=o0v[i][:, a:b, :], in_=outs[i][:, a:b, :])
+
+        dws = {}
+        part = {}
+
+        def dw(lo, hi, m, h):
+            dws[lo, m, h] = pt("mm", 3)
+            for i in range(lo, hi):
+                s = 2 * i + h
+                nc.tensor.matmul_mx(out=dws[lo, m, h][:], lhsT=ec[i][:, P * m:P * (m + 1)].bitcast(E4M3), lhsT_scale=es[i][:, P * m:P * (m + 1)],
+                                    rhs=dzc[s][:].bitcast(E5M2), rhs_scale=dzs[s][:], start=(i == lo), stop=(i == hi - 1))
+
+        def dw_park(m, h):
+            if h == 0 and m % 2 == 0:
+                part[m] = st([P, 2, 1024], F32, "part", "z1t", 5)
+                part[m + 1] = part[m]
+            nc.scalar.copy(out=part[m][:, m % 2, 512 * h:512 * (h + 1)].rearrange("p (q t) -> p q t", t=4), in_=dws[0, m, h][:].rearrange("p (t q) -> p q t", t=4))
+
+        def dw_add(m, h):
+            dst = part[m][:, m % 2, 512 * h:512 * (h + 1)]
+            nc.vector.tensor_tensor(out=dst.rearrange("p (q t) -> p q t", t=4), in0=dws[SPLIT, m, h][:].rearrange("p (t q) -> p q t", t=4),
+                                    in1=dst.rearrange("p (q t) -> p q t", t=4), op=ALU.add)
+            nc.sync.dma_start(out=out_1[P * m:P * (m + 1), 512 * h:512 * (h + 1)], in_=dst)
+
+        vcopy = nc.vector.tensor_copy
+        scopy = nc.scalar.copy
+
+        dz2_values(0, 1)
+        tp0 = dz2_turn(0)
+        dz2_copy(0, tp0)
+        tpa = wa_turn(0, 0)
+        tpb = wa_turn(0, 1)
+        dz2_quant(0, 1)
+        wa_copy(vcopy, 0, 0, tpa)
+        wa_copy(scopy, 0, 1, tpb)
+        wa_quant(0)
+        dagg(0)
+        mask(0)
+        for b in range(2):
+            wa_copy(scopy, 1, b, wa_turn(1, b))
+
+        dw_jobs = [(m, h) for h in range(2) for m in range(4)]
+        for s in range(HALVES):
+            i, g = s // 2, s % 2
+            if s + 5 < HALVES:
+                load_z1(s + 5)
+            if g == 0 and 1 <= i < GROUPS - 1:
+                load_e2(i + 1)
+            done = (s - 3) // 2
+            if s >= 3:
+                for j in ((0, 1) if s % 2 == 1 else (2, 3)):
+                    de2(done, j)
+                    de2_copy(scopy, done, j)
+                if s % 2 == 0:
+                    store(done, 0, 4)
+            e2_copy(i, g)
+            if g == 0 and i > 0:
+                e2_quant(i - 1)
+            if s >= 10:
+                for m, h in dw_jobs[:2 if s % 3 == 1 else 1]:
+                    dw(0, SPLIT, m, h)
+                    dw_park(m, h)
+                dw_jobs = dw_jobs[2 if s % 3 == 1 else 1:]
+            product(s)
+            turn(s)
+            if s == 0:
+                wa_quant(1)
+                dagg(1)
+            if s + 1 < HALVES:
+                mask(s + 1)
+            if s > 0:
+                quant_feats(s - 1)
+            quant_edges(s)
+            untangle(scopy, s, 0)
+            untangle(scopy, s, 1)
+            if s == 0:
+                dz2_values(1, 4)
+            if s == 1:
+                for n in range(1, 4):
+                    dz2_copy(n, dz2_turn(n))
+                dz2_quant(1, 2)
+                dz2_quant(2, 4)
+                for b in range(2):
+                    fe_copy(scopy, 0, b, fe_turn(0, b))
+            if s == 2:
+                fe_quant(0)
+                for b in range(2):
+                    fe_copy(scopy, 1, b, fe_turn(1, b))
+            if s + 2 < HALVES:
+                dagg(s + 2)
+            if s == 2:
+                fe_quant(1)
+
+        e2_quant(7)
+        for j in (2, 3):
+            de2(6, j)
+            de2_copy(scopy, 6, j)
+        store(6, 0, 4)
+        quant_feats(15)
+        for m in range(4):
+            dw(SPLIT, GROUPS, m, 0)
+            dw_add(m, 0)
+        for j in range(4):
+            de2(7, j)
+            de2_copy(scopy, 7, j)
+            store(7, j, j + 1)
+        for m in range(4):
+            dw(SPLIT, GROUPS, m, 1)
+            dw_add(m, 1)

@@ -16,9 +16,405 @@ BYTES = 2 * (4096 * 512 + 2 * 512 * 1024 + 512 * 512) + 4 * (4096 * 1024 + 512 *
 
 P = 128
 GROUPS = 8
-HALVES = 16
+STEPS = 16
 SLOPE = 0.2
-SPLIT = 5
+PARKED = 5
+SIGNED = (1, 2, 3, 4, 5, 6, 7, 8, 10, 12, 13, 14)
+GE = (1, 2, 3, 4, 5, 6, 7)
+DZC_BUFS = (3, 8)
+DTC_BUFS = (4, 3)
+ON_VECTOR = (
+    ("w_copy", "wa", 0, 1),
+    ("de2_copy", 0, 0),
+    ("de2_copy", 0, 2),
+    ("untangle", 2, 0),
+    ("de2_copy", 0, 3),
+    ("de2_copy", 1, 2),
+    ("de2_copy", 2, 2),
+    ("de2_copy", 2, 3),
+    ("dw_park", 0),
+    ("dw_park", 2),
+    ("de2_copy", 3, 0),
+    ("de2_copy", 3, 1),
+    ("untangle", 13, 0),
+    ("dw_out", 0, 1),
+    ("dw_out", 0, 3),
+    ("untangle", 7, 0),
+    ("untangle", 15, 0),
+    ("de2_copy", 7, 3),
+    ("de2_copy", 7, 1),
+    ("de2_copy", 7, 2),
+)
+ORDER = (
+    ("load_nodes", 0, 1),
+    ("load_nodes", 1, 4),
+    ("load_wa", 0),
+    ("load_z1", 0, 0, 1),
+    ("load_e2", 0),
+    ("load_wa", 1),
+    ("load_z1", 0, 1, 2),
+    ("load_z1", 1, 0, 2),
+    ("load_fe",),
+    ("dz2_values", 0, 1),
+    ("dz2_turn", 0),
+    ("dz2_copy", 0),
+    ("dz2_quant", 0),
+    ("load_z1", 2, 0, 2),
+    ("dz2_values", 2, 4),
+    ("w_turn", "wa", 0, 0),
+    ("w_turn", "wa", 0, 1),
+    ("dz2_values", 1, 2),
+    ("w_copy", "wa", 0, 0),
+    ("dz2_turn", 3),
+    ("load_e2", 1),
+    ("dz2_turn", 2),
+    ("dz2_copy", 3),
+    ("w_copy", "wa", 0, 1),
+    ("dz2_copy", 2),
+    ("dz2_turn", 1),
+    ("dz2_quant", 3),
+    ("w_quant", "wa", 0),
+    ("dz2_copy", 1),
+    ("mask", 0),
+    ("dagg", 0),
+    ("e2_copy", 0, 0),
+    ("dz2_quant", 1),
+    ("product", 0),
+    ("w_turn", "wa", 1, 0),
+    ("e2_copy", 0, 1),
+    ("w_turn", "wa", 1, 1),
+    ("w_copy", "wa", 1, 0),
+    ("load_e2", 2),
+    ("load_e2", 3),
+    ("w_copy", "wa", 1, 1),
+    ("e2_quant", 0),
+    ("turn", 0, 0),
+    ("mask", 8),
+    ("w_quant", "wa", 1),
+    ("turn", 0, 1),
+    ("quant_edges", 0),
+    ("dagg", 8),
+    ("dz2_quant", 2),
+    ("dw", 0, 1),
+    ("dw", 0, 0),
+    ("dw", 0, 3),
+    ("dw", 0, 2),
+    ("untangle", 0, 0),
+    ("load_z1", 3, 0, 2),
+    ("product", 8),
+    ("untangle", 0, 1),
+    ("mask", 1),
+    ("quant_feats", 0),
+    ("turn", 8, 1),
+    ("mask", 9),
+    ("turn", 8, 0),
+    ("dagg", 1),
+    ("quant_edges", 8),
+    ("untangle", 8, 0),
+    ("w_turn", "fe", 0, 0),
+    ("load_z1", 4, 0, 2),
+    ("product", 1),
+    ("untangle", 8, 1),
+    ("w_turn", "fe", 0, 1),
+    ("w_copy", "fe", 0, 0),
+    ("w_turn", "fe", 1, 0),
+    ("quant_feats", 8),
+    ("w_copy", "fe", 0, 1),
+    ("w_turn", "fe", 1, 1),
+    ("quant_edges", 1),
+    ("w_copy", "fe", 1, 0),
+    ("turn", 1, 0),
+    ("w_quant", "fe", 0),
+    ("w_copy", "fe", 1, 1),
+    ("dagg", 9),
+    ("untangle", 1, 0),
+    ("turn", 1, 1),
+    ("w_quant", "fe", 1),
+    ("product", 9),
+    ("de2", 0, 0),
+    ("mask", 2),
+    ("e2_copy", 1, 0),
+    ("de2", 0, 2),
+    ("de2_copy", 0, 0),
+    ("e2_copy", 1, 1),
+    ("dagg", 2),
+    ("mask", 10),
+    ("de2_copy", 0, 2),
+    ("turn", 9, 1),
+    ("product", 2),
+    ("turn", 9, 0),
+    ("load_e2", 4),
+    ("untangle", 1, 1),
+    ("load_z1", 5, 0, 2),
+    ("e2_quant", 1),
+    ("dagg", 10),
+    ("quant_edges", 2),
+    ("untangle", 9, 0),
+    ("dw", 1, 3),
+    ("dw", 1, 1),
+    ("quant_feats", 1),
+    ("turn", 2, 1),
+    ("e2_copy", 2, 0),
+    ("product", 10),
+    ("untangle", 9, 1),
+    ("de2", 0, 1),
+    ("dw", 1, 2),
+    ("mask", 3),
+    ("turn", 2, 0),
+    ("e2_copy", 2, 1),
+    ("dw", 1, 0),
+    ("untangle", 2, 0),
+    ("dagg", 3),
+    ("load_e2", 5),
+    ("quant_feats", 9),
+    ("turn", 10, 0),
+    ("untangle", 2, 1),
+    ("product", 3),
+    ("untangle", 10, 0),
+    ("de2", 1, 0),
+    ("de2_copy", 0, 1),
+    ("de2", 0, 3),
+    ("mask", 11),
+    ("de2_copy", 1, 0),
+    ("turn", 3, 1),
+    ("mask", 4),
+    ("dagg", 11),
+    ("quant_feats", 2),
+    ("turn", 3, 0),
+    ("load_z1", 6, 0, 2),
+    ("e2_quant", 2),
+    ("quant_edges", 3),
+    ("dw", 2, 1),
+    ("dw", 2, 3),
+    ("de2_copy", 0, 3),
+    ("e2_copy", 3, 0),
+    ("untangle", 3, 0),
+    ("dw", 2, 0),
+    ("dw", 2, 2),
+    ("product", 11),
+    ("store", 0, 0, 4),
+    ("turn", 10, 1),
+    ("untangle", 3, 1),
+    ("de2", 1, 2),
+    ("e2_copy", 3, 1),
+    ("untangle", 10, 1),
+    ("de2", 1, 1),
+    ("de2_copy", 1, 2),
+    ("dagg", 4),
+    ("load_e2", 6),
+    ("quant_edges", 10),
+    ("mask", 12),
+    ("turn", 11, 1),
+    ("e2_quant", 3),
+    ("turn", 11, 0),
+    ("quant_feats", 10),
+    ("dw", 3, 2),
+    ("dw", 3, 3),
+    ("quant_feats", 3),
+    ("dw", 3, 0),
+    ("dw", 3, 1),
+    ("quant_edges", 11),
+    ("de2_copy", 1, 1),
+    ("load_z1", 7, 0, 2),
+    ("quant_edges", 9),
+    ("untangle", 11, 0),
+    ("de2", 2, 0),
+    ("e2_copy", 4, 0),
+    ("product", 4),
+    ("de2_copy", 2, 0),
+    ("de2", 1, 3),
+    ("untangle", 11, 1),
+    ("de2", 2, 2),
+    ("e2_copy", 4, 1),
+    ("de2_copy", 2, 2),
+    ("de2_copy", 1, 3),
+    ("dagg", 12),
+    ("turn", 4, 0),
+    ("mask", 5),
+    ("product", 12),
+    ("store", 1, 0, 4),
+    ("load_e2", 7),
+    ("de2", 2, 3),
+    ("turn", 4, 1),
+    ("e2_quant", 4),
+    ("untangle", 4, 0),
+    ("dagg", 5),
+    ("quant_edges", 12),
+    ("quant_edges", 4),
+    ("untangle", 4, 1),
+    ("dw_early", 1),
+    ("quant_feats", 11),
+    ("mask", 13),
+    ("e2_copy", 5, 0),
+    ("product", 5),
+    ("dw", 4, 0),
+    ("dw_early", 0),
+    ("e2_copy", 5, 1),
+    ("de2_copy", 2, 3),
+    ("dw", 4, 2),
+    ("dw_park", 1),
+    ("dagg", 13),
+    ("dw_park", 0),
+    ("dw", 4, 3),
+    ("mask", 6),
+    ("turn", 5, 1),
+    ("product", 13),
+    ("turn", 5, 0),
+    ("dw_early", 2),
+    ("untangle", 5, 0),
+    ("e2_quant", 5),
+    ("dagg", 6),
+    ("quant_edges", 5),
+    ("dw", 4, 1),
+    ("untangle", 5, 1),
+    ("de2", 3, 0),
+    ("quant_feats", 4),
+    ("dw", 5, 1),
+    ("dw_park", 2),
+    ("e2_copy", 6, 0),
+    ("dw", 5, 0),
+    ("mask", 14),
+    ("turn", 12, 1),
+    ("de2_copy", 3, 0),
+    ("product", 6),
+    ("turn", 12, 0),
+    ("e2_copy", 6, 1),
+    ("dw_early", 3),
+    ("untangle", 12, 0),
+    ("dw", 5, 2),
+    ("quant_feats", 5),
+    ("dw", 5, 3),
+    ("untangle", 12, 1),
+    ("quant_edges", 6),
+    ("de2", 3, 2),
+    ("e2_quant", 6),
+    ("dagg", 14),
+    ("dw_park", 3),
+    ("de2", 3, 3),
+    ("product", 14),
+    ("e2_copy", 7, 0),
+    ("de2_copy", 3, 2),
+    ("turn", 13, 1),
+    ("de2_copy", 3, 3),
+    ("dw", 6, 1),
+    ("mask", 7),
+    ("de2", 3, 1),
+    ("e2_copy", 7, 1),
+    ("turn", 13, 0),
+    ("de2_copy", 3, 1),
+    ("dw", 6, 0),
+    ("untangle", 13, 0),
+    ("store", 3, 0, 4),
+    ("dagg", 7),
+    ("de2", 2, 1),
+    ("untangle", 13, 1),
+    ("dw", 6, 2),
+    ("quant_feats", 12),
+    ("turn", 6, 0),
+    ("quant_edges", 13),
+    ("de2_copy", 2, 1),
+    ("de2", 4, 0),
+    ("quant_feats", 13),
+    ("untangle", 6, 0),
+    ("store", 2, 0, 4),
+    ("de2", 4, 2),
+    ("product", 7),
+    ("dw", 6, 3),
+    ("de2_copy", 4, 0),
+    ("de2", 4, 3),
+    ("de2_copy", 4, 2),
+    ("de2", 4, 1),
+    ("de2_copy", 4, 3),
+    ("turn", 6, 1),
+    ("e2_quant", 7),
+    ("de2_copy", 4, 1),
+    ("turn", 14, 0),
+    ("quant_edges", 7),
+    ("untangle", 6, 1),
+    ("store", 4, 0, 4),
+    ("turn", 14, 1),
+    ("mask", 15),
+    ("dw", 7, 3),
+    ("untangle", 14, 0),
+    ("dw", 7, 1),
+    ("de2", 5, 0),
+    ("dw_out", 0, 1),
+    ("dw", 7, 0),
+    ("untangle", 14, 1),
+    ("quant_edges", 14),
+    ("dw", 7, 2),
+    ("dw_store", 0, 1),
+    ("dagg", 15),
+    ("quant_feats", 6),
+    ("de2", 5, 3),
+    ("dw_out", 0, 2),
+    ("dw", 13, 1),
+    ("quant_feats", 14),
+    ("dw", 14, 1),
+    ("de2_copy", 5, 0),
+    ("dw_store", 0, 2),
+    ("de2", 5, 2),
+    ("product", 15),
+    ("de2_copy", 5, 3),
+    ("de2", 5, 1),
+    ("de2_copy", 5, 2),
+    ("de2", 6, 0),
+    ("de2_copy", 5, 1),
+    ("de2", 6, 1),
+    ("de2_copy", 6, 0),
+    ("dw_out", 0, 3),
+    ("store", 5, 0, 4),
+    ("de2", 6, 2),
+    ("de2_copy", 6, 1),
+    ("quant_edges", 15),
+    ("turn", 7, 0),
+    ("dw_store", 0, 3),
+    ("de2_copy", 6, 2),
+    ("turn", 7, 1),
+    ("dw_out", 0, 0),
+    ("untangle", 7, 0),
+    ("dw", 15, 1),
+    ("untangle", 7, 1),
+    ("de2", 6, 3),
+    ("dw_store", 0, 0),
+    ("dw_out", 1, 1),
+    ("dw", 13, 2),
+    ("turn", 15, 0),
+    ("de2_copy", 6, 3),
+    ("dw_store", 1, 1),
+    ("quant_feats", 7),
+    ("turn", 15, 1),
+    ("store", 6, 0, 4),
+    ("untangle", 15, 0),
+    ("dw", 14, 2),
+    ("untangle", 15, 1),
+    ("dw", 15, 2),
+    ("dw", 13, 0),
+    ("dw", 13, 3),
+    ("dw_out", 1, 2),
+    ("dw", 14, 3),
+    ("dw", 15, 3),
+    ("quant_feats", 15),
+    ("dw_store", 1, 2),
+    ("dw", 14, 0),
+    ("dw", 15, 0),
+    ("dw_out", 1, 3),
+    ("de2", 7, 0),
+    ("dw_out", 1, 0),
+    ("dw_store", 1, 3),
+    ("de2", 7, 3),
+    ("de2_copy", 7, 0),
+    ("dw_store", 1, 0),
+    ("de2", 7, 1),
+    ("de2_copy", 7, 3),
+    ("store", 7, 0, 1),
+    ("de2", 7, 2),
+    ("de2_copy", 7, 1),
+    ("store", 7, 3, 4),
+    ("de2_copy", 7, 2),
+    ("store", 7, 1, 2),
+    ("store", 7, 2, 3),
+)
 
 
 def tile_graph_gan_pb_v_kernel(tc, e2, x, fe_w2, fe_b2, fn_w0, fn_b0, z1, z2, grad_out, out_0, out_1):
@@ -35,6 +431,9 @@ def tile_graph_gan_pb_v_kernel(tc, e2, x, fe_w2, fe_b2, fn_w0, fn_b0, z1, z2, gr
             t = ps.tile([P, 512], F32, name=tag, tag=tag, bufs=bufs)
             return t
 
+        def copier(*job):
+            return nc.vector.tensor_copy if job in ON_VECTOR else nc.scalar.copy
+
         z1v = z1.flatten_outer_dims().rearrange("(i p j) w -> i p j w", p=P, j=4)
         e2v = e2.flatten_outer_dims().rearrange("(i p j) f -> i p j f", p=P, j=4)
         o0v = out_0.flatten_outer_dims().rearrange("(i p j) f -> i p j f", p=P, j=4)
@@ -46,85 +445,90 @@ def tile_graph_gan_pb_v_kernel(tc, e2, x, fe_w2, fe_b2, fn_w0, fn_b0, z1, z2, gr
         ident = st([P, P], F32, "ident", "ident", 1)
         make_identity(nc, ident[:])
 
-        z2t = st([P, 4, 512], F32, "z2t", "io8", 3)
-        got = st([P, 4, 512], BF16, "got", "dz", 3)
-        nc.sync.dma_start(out=z2t[:, 0, :], in_=z2v[:, 0, :])
-        nc.sync.dma_start(out=got[:, 0, :], in_=gov[:, 0, :])
-        wa_raw = st([P, 2, 4, 512], BF16, "wa_raw", "io8", 3)
-        nc.sync.dma_start(out=wa_raw[:, 0], in_=wav[0])
-
         z1t = {}
         e2t = {}
+        wa_raw = {}
+        z2t = st([P, 4, 512], F32, "z2t", "io8", 3)
+        got = st([P, 4, 512], BF16, "got", "n4", 2)
+        dz2 = st([P, 4, 512], BF16, "dz2", "n4", 2)
+        fe_raw = {}
 
-        def load_z1(s):
-            z1t[s] = st([P, 4, 512], F32, "z1t", "z1t", 5)
-            g = s % 2
-            nc.sync.dma_start(out=z1t[s][:], in_=z1v[s // 2][:, :, 512 * g:512 * (g + 1)])
+        def load_z1(i, a, b):
+            if i not in z1t:
+                z1t[i] = st([P, 4096], F32, "z1t", "z1t", 3)
+            if i == 0:
+                dst = z1t[i][:, 2048 * a:2048 * b].rearrange("p (j w) -> p j w", j=4)
+            else:
+                dst = z1t[i][:].rearrange("p (j w) -> p j w", j=4)
+            nc.sync.dma_start(out=dst, in_=z1v[i][:, :, 512 * a:512 * b])
 
         def load_e2(i):
-            e2t[i] = st([P, 4, 512], BF16, "e2t", "e2t", 2)
+            e2t[i] = st([P, 4, 512], BF16, "e2t", "k4", 3)
             nc.sync.dma_start(out=e2t[i][:], in_=e2v[i])
 
-        load_z1(0)
-        nc.sync.dma_start(out=wa_raw[:, 1], in_=wav[1])
-        load_z1(1)
-        nc.sync.dma_start(out=z2t[:, 1:4, :], in_=z2v[:, 1:4, :])
-        nc.sync.dma_start(out=got[:, 1:4, :], in_=gov[:, 1:4, :])
-        load_e2(0)
-        load_z1(2)
-        fe_raw = st([P, 4, 1024], BF16, "fe_raw", "io8", 3)
-        nc.sync.dma_start(out=fe_raw[:], in_=fev)
-        load_z1(3)
-        load_e2(1)
-        load_z1(4)
+        def load_wa(h):
+            wa_raw[h] = st([P, 4, 512], BF16, "wa_raw", "k4", 3)
+            nc.sync.dma_start(out=wa_raw[h][:], in_=wav[h])
 
-        dz2 = st([P, 4, 512], BF16, "dz2", "dz", 3)
-        dz2_t = st([P, 4096], BF16, "dz2_t", "turned", 1)
-        dz2_c = st([P, 1024], U32, "dz2_c", "dz2_c", 1)
-        dz2_s = st([P, 1024], U8, "dz2_s", "dz2_s", 1)
+        def load_fe():
+            fe_raw[0] = st([P, 4, 1024], BF16, "fe_raw", "io8", 3)
+            nc.sync.dma_start(out=fe_raw[0][:], in_=fev)
+
+        def load_nodes(a, b):
+            nc.sync.dma_start(out=z2t[:, a:b, :], in_=z2v[:, a:b, :])
+            nc.sync.dma_start(out=got[:, a:b, :], in_=gov[:, a:b, :])
+
+        banks = {}
+        dz2_t = {}
+        dz2_c = {}
+        dz2_s = {}
 
         def dz2_values(a, b):
             nc.vector.tensor_scalar(out=z2t[:, a:b, :], in0=z2t[:, a:b, :], scalar1=0.0, scalar2=SLOPE, op0=ALU.is_gt, op1=ALU.max)
             nc.vector.tensor_tensor(out=dz2[:, a:b, :], in0=got[:, a:b, :], in1=z2t[:, a:b, :], op=ALU.mult)
 
         def dz2_turn(n):
-            tp = pt("tp", 3)
+            banks["dz2", n] = pt("w", 3)
             words = dz2[:, n, :].bitcast(F32)
             for u in range(2):
-                nc.tensor.transpose(tp[:, P * u:P * (u + 1)], words[:, u:256:2], ident[:])
-            return tp
+                nc.tensor.transpose(banks["dz2", n][:, P * u:P * (u + 1)], words[:, u:256:2], ident[:])
 
-        def dz2_copy(n, tp):
-            dst = dz2_t[:].bitcast(F32)[:, 512 * n:512 * (n + 1)].rearrange("p (n d u) -> p n d u", d=2, u=2)
-            src = tp[:, 0:256].rearrange("p (u n) -> p n u", u=2).unsqueeze(2).to_broadcast([P, P, 2, 2])
-            nc.vector.tensor_copy(out=dst, in_=src)
+        def dz2_copy(n):
+            dz2_t[n] = st([P, 1024], BF16, "dz2_t", "dz2_t", 2)
+            dst = dz2_t[n][:].bitcast(F32).rearrange("p (n d u) -> p n d u", d=2, u=2)
+            src = banks["dz2", n][:, 0:256].rearrange("p (u n) -> p n u", u=2).unsqueeze(2).to_broadcast([P, P, 2, 2])
+            copier("dz2_copy", n)(out=dst, in_=src)
 
-        def dz2_quant(a, b):
-            nc.vector.quantize_mx(out=dz2_c[:, 256 * a:256 * b].bitcast(E5M2), scales=dz2_s[:, 256 * a:256 * b], in_=dz2_t[:, 1024 * a:1024 * b])
+        def dz2_quant(n):
+            dz2_c[n] = st([P, 256], U32, "dz2_c", "dz2_c", 4)
+            dz2_s[n] = st([P, 256], U8, "dz2_s", "dz2_s", 4)
+            nc.vector.quantize_mx(out=dz2_c[n][:].bitcast(E5M2), scales=dz2_s[n][:], in_=dz2_t[n][:])
 
-        def turn_words(words, bank_cols, tp):
-            for k, (row, lo) in enumerate(bank_cols):
-                nc.tensor.transpose(tp[:, P * k:P * (k + 1)], words[row][:, lo:lo + 255:2], ident[:])
+        w_g = {}
+        w_c = {}
+        w_s = {}
 
-        def copy_words(eng_copy, dst_words, tp):
-            eng_copy(out=dst_words.rearrange("p (s m u) -> p s m u", s=2, u=2), in_=tp[:].rearrange("p (s u m) -> p s m u", s=2, u=2))
+        def w_turn(w, h, b):
+            banks[w, h, b] = pt("w", 3)
+            for s in range(2):
+                for u in range(2):
+                    r = 2 * b + s
+                    if w == "wa":
+                        words = wa_raw[h][:, r, :].bitcast(F32)[:, u:256:2]
+                    else:
+                        words = fe_raw[0][:, r, :].bitcast(F32)[:, 256 * h + u:256 * (h + 1):2]
+                    nc.tensor.transpose(banks[w, h, b][:, P * (2 * s + u):P * (2 * s + u + 1)], words, ident[:])
 
-        wa_g = st([P, 4096], BF16, "wa_g", "mk", 3)
-        wa_c = st([P, 1024], U32, "wa_c", "wa_c", 1)
-        wa_s = st([P, 1024], U8, "wa_s", "wa_s", 1)
+        def w_copy(w, h, b):
+            if (w, h) not in w_g:
+                w_g[w, h] = st([P, 2048], BF16, "w_g", "w_g", 2)
+            words = w_g[w, h][:].bitcast(F32)[:, 512 * b:512 * (b + 1)]
+            copier("w_copy", w, h, b)(out=words.rearrange("p (s m u) -> p s m u", s=2, u=2), in_=banks[w, h, b][:].rearrange("p (s u m) -> p s m u", s=2, u=2))
 
-        def wa_turn(g, b):
-            tp = pt("tp", 3)
-            words = [wa_raw[:, g, t, :].bitcast(F32) for t in range(4)]
-            turn_words(words, [(2 * b + s, u) for s in range(2) for u in range(2)], tp)
-            return tp
-
-        def wa_copy(eng_copy, g, b, tp):
-            c0 = 1024 * g + 512 * b
-            copy_words(eng_copy, wa_g[:].bitcast(F32)[:, c0:c0 + 512], tp)
-
-        def wa_quant(g):
-            nc.vector.quantize_mx(out=wa_c[:, 512 * g:512 * (g + 1)].bitcast(E4M3), scales=wa_s[:, 512 * g:512 * (g + 1)], in_=wa_g[:, 2048 * g:2048 * (g + 1)])
+        def w_quant(w, h):
+            w_c[w, h] = st([P, 512], U32, "w_c", "w_c", 4)
+            w_s[w, h] = st([P, 512], U8, "w_s", "w_s", 4)
+            nc.vector.quantize_mx(out=w_c[w, h][:].bitcast(E4M3), scales=w_s[w, h][:], in_=w_g[w, h][:])
 
         d_ps = {}
         mk = {}
@@ -134,205 +538,137 @@ def tile_graph_gan_pb_v_kernel(tc, e2, x, fe_w2, fe_b2, fn_w0, fn_b0, z1, z2, gr
         dzt = {}
         dtc = {}
         dts = {}
-        tps = {}
 
-        def dagg(s):
-            i, g = s // 2, s % 2
-            d_ps[s] = pt("d", 2)
-            nc.tensor.matmul_mx(out=d_ps[s][:], lhsT=dz2_c[:, P * i:P * (i + 1)].bitcast(E5M2), lhsT_scale=dz2_s[:, P * i:P * (i + 1)],
-                                rhs=wa_c[:, 512 * g:512 * (g + 1)].bitcast(E4M3), rhs_scale=wa_s[:, 512 * g:512 * (g + 1)], start=True, stop=True)
+        def dagg(k):
+            h, i = k // GROUPS, k % GROUPS
+            d_ps[k] = pt("d", 1)
+            cols = slice(P * (i % 2), P * (i % 2 + 1))
+            nc.tensor.matmul_mx(out=d_ps[k][:], lhsT=dz2_c[i // 2][:, cols].bitcast(E5M2), lhsT_scale=dz2_s[i // 2][:, cols],
+                                rhs=w_c["wa", h][:].bitcast(E4M3), rhs_scale=w_s["wa", h][:], start=True, stop=True)
 
-        def mask(s):
-            mk[s] = st([P, 4, 512], F32, "mk", "mk", 3)
-            nc.vector.tensor_scalar(out=mk[s][:].rearrange("p j (t q) -> p j q t", t=4), in0=z1t[s][:].rearrange("p j (q t) -> p j q t", t=4),
-                                    scalar1=0.0, scalar2=SLOPE, op0=ALU.is_gt, op1=ALU.max)
+        def mask(k):
+            mk[k] = st([P, 2048], F32, "mk", "mk", 2)
+            out = mk[k][:].rearrange("p (t q j) -> p q j t", t=4, j=4)
+            h, i = k // GROUPS, k % GROUPS
+            if i == 0:
+                z = z1t[i][:, 2048 * h:2048 * (h + 1)].rearrange("p (j q t) -> p q j t", j=4, t=4)
+            else:
+                z = z1t[i][:].rearrange("p (j h q t) -> p h q j t", j=4, h=2, t=4)[:, h]
+            if k in SIGNED:
+                nc.scalar.activation(out=out, in_=z, func=mybir.ActivationFunctionType.Sign)
+            else:
+                nc.vector.tensor_scalar(out=out, in0=z, scalar1=0.0, scalar2=SLOPE, op0=ALU.is_gt, op1=ALU.max)
 
-        def product(s):
-            dz[s] = st([P, 2048], BF16, "dz", "dz", 3)
-            nc.vector.tensor_tensor(out=dz[s][:].rearrange("p (c i j) -> p c j i", i=2, j=4), in0=mk[s][:].rearrange("p j (c i) -> p c j i", i=2),
-                                    in1=d_ps[s][:].rearrange("p (c i) -> p c i", i=2).unsqueeze(2).to_broadcast([P, 256, 4, 2]), op=ALU.mult)
+        def product(k):
+            dz[k] = st([P, 2048], BF16, "dz", "dz", 3)
+            out = dz[k][:].rearrange("p (c j) -> p c j", j=4)
+            slope = mk[k][:].rearrange("p (c j) -> p c j", j=4)
+            grad = d_ps[k][:].unsqueeze(2).to_broadcast([P, 512, 4])
+            if k in SIGNED:
+                nc.vector.scalar_tensor_tensor(out=out, in0=slope, scalar=SLOPE, in1=grad, op0=ALU.max, op1=ALU.mult)
+            else:
+                nc.vector.tensor_tensor(out=out, in0=slope, in1=grad, op=ALU.mult)
 
-        def quant_edges(s):
-            dzc[s] = st([P, 512], U32, "dzc", "dzc", HALVES)
-            dzs[s] = st([P, 512], U8, "dzs", "dzs", HALVES)
-            nc.vector.quantize_mx(out=dzc[s][:].bitcast(E5M2), scales=dzs[s][:], in_=dz[s][:])
+        def quant_edges(k):
+            h = k // GROUPS
+            dzc[k] = st([P, 512], U32, "dzc", "dzc%d" % h, DZC_BUFS[h])
+            dzs[k] = st([P, 512], U8, "dzs", "dzs%d" % h, DZC_BUFS[h])
+            nc.vector.quantize_mx(out=dzc[k][:].bitcast(E5M2), scales=dzs[k][:], in_=dz[k][:])
 
-        def turn(s):
-            words = dz[s][:].bitcast(F32)
-            tps[s] = []
-            for h in range(2):
-                tp = pt("tp", 3)
-                for t in range(4):
-                    nc.tensor.transpose(tp[:, P * t:P * (t + 1)], words[:, 256 * t + h:256 * (t + 1):2], ident[:])
-                tps[s].append(tp)
+        def turn(k, u):
+            words = dz[k][:].bitcast(F32)
+            banks["dz", k, u] = pt("w", 3)
+            for t in range(4):
+                nc.tensor.transpose(banks["dz", k, u][:, P * t:P * (t + 1)], words[:, 256 * t + u:256 * (t + 1):2], ident[:])
 
-        def untangle(eng_copy, s, h):
-            if h == 0:
-                dzt[s] = st([P, 2048], BF16, "dzt", "dzt", 3)
-            eng_copy(out=dzt[s][:, 1024 * h:1024 * (h + 1)].rearrange("p (e n t) -> p e n t", e=2, t=4),
-                     in_=tps[s][h][:].bitcast(BF16).rearrange("p (t n e) -> p e n t", t=4, e=2))
+        def untangle(k, u):
+            if k not in dzt:
+                dzt[k] = st([P, 2048], BF16, "dzt", "dzt", 2)
+            copier("untangle", k, u)(out=dzt[k][:, 1024 * u:1024 * (u + 1)].rearrange("p (e n t) -> p e n t", e=2, t=4),
+                                     in_=banks["dz", k, u][:].bitcast(BF16).rearrange("p (t n e) -> p e n t", t=4, e=2))
 
-        def quant_feats(s):
-            dtc[s] = st([P, 512], U32, "dtc", "dtc", 4)
-            dts[s] = st([P, 512], U8, "dts", "dts", 4)
-            nc.vector.quantize_mx(out=dtc[s][:].bitcast(E5M2), scales=dts[s][:], in_=dzt[s][:])
+        def quant_feats(k):
+            h = k // GROUPS
+            dtc[k] = st([P, 512], U32, "dtc", "dtc%d" % h, DTC_BUFS[h])
+            dts[k] = st([P, 512], U8, "dts", "dts%d" % h, DTC_BUFS[h])
+            nc.vector.quantize_mx(out=dtc[k][:].bitcast(E5M2), scales=dts[k][:], in_=dzt[k][:])
 
         eg = {}
         ec = {}
         es = {}
 
-        def e2_copy(i, h):
-            if h == 0:
-                eg[i] = st([P, 2048], BF16, "eg", "eg", 2)
-            nc.scalar.copy(out=eg[i][:, 1024 * h:1024 * (h + 1)].rearrange("p (c i j) -> p c j i", i=4, j=4),
-                           in_=e2t[i][:, :, 256 * h:256 * (h + 1)].rearrange("p j (c i) -> p c j i", i=4))
+        def e2_copy(i, b):
+            if i not in eg:
+                eg[i] = st([P, 2048], BF16, "eg", "eg", 1)
+            lo = 256 * b
+            dst = eg[i][:, 4 * lo:4 * lo + 1024]
+            if i in GE:
+                for c in (0, 128):
+                    nc.gpsimd.tensor_scalar(out=dst[:, 4 * c:4 * c + 512].rearrange("p (c j) -> p c j", j=4), in0=e2t[i][:, :, lo + c:lo + c + 128].rearrange("p j c -> p c j"),
+                                            scalar1=1.0, scalar2=0.0, op0=ALU.mult, op1=ALU.add)
+            else:
+                nc.scalar.copy(out=dst.rearrange("p (c i j) -> p c j i", i=4, j=4), in_=e2t[i][:, :, lo:lo + 256].rearrange("p j (c i) -> p c j i", i=4))
 
         def e2_quant(i):
             ec[i] = st([P, 512], U32, "ec", "ec", GROUPS)
             es[i] = st([P, 512], U8, "es", "es", GROUPS)
             nc.vector.quantize_mx(out=ec[i][:].bitcast(E4M3), scales=es[i][:], in_=eg[i][:])
 
-        fe_gs = []
-        fe_c = st([P, 1024], U32, "fe_c", "fe_c", 1)
-        fe_s = st([P, 1024], U8, "fe_s", "fe_s", 1)
-
-        def fe_turn(g, b):
-            if not fe_gs:
-                fe_gs.append(st([P, 4096], BF16, "fe_g", "turned", 1))
-            tp = pt("tp", 3)
-            words = [fe_raw[:, r, :].bitcast(F32) for r in range(4)]
-            turn_words(words, [(2 * b + r, 256 * g + u) for r in range(2) for u in range(2)], tp)
-            return tp
-
-        def fe_copy(eng_copy, g, b, tp):
-            c0 = 1024 * g + 512 * b
-            copy_words(eng_copy, fe_gs[0][:].bitcast(F32)[:, c0:c0 + 512], tp)
-
-        def fe_quant(g):
-            nc.vector.quantize_mx(out=fe_c[:, 512 * g:512 * (g + 1)].bitcast(E4M3), scales=fe_s[:, 512 * g:512 * (g + 1)], in_=fe_gs[0][:, 2048 * g:2048 * (g + 1)])
-
-        mms = {}
         outs = {}
+        parts = {}
 
         def de2(i, j):
-            mms[i, j] = pt("mm", 3)
-            for g in range(2):
-                s = 2 * i + g
-                nc.tensor.matmul_mx(out=mms[i, j][:], lhsT=dtc[s][:, P * j:P * (j + 1)].bitcast(E5M2), lhsT_scale=dts[s][:, P * j:P * (j + 1)],
-                                    rhs=fe_c[:, 512 * g:512 * (g + 1)].bitcast(E4M3), rhs_scale=fe_s[:, 512 * g:512 * (g + 1)], start=(g == 0), stop=(g == 1))
+            banks["de2", i, j] = pt("w", 3)
+            for h in range(2):
+                k = GROUPS * h + i
+                nc.tensor.matmul_mx(out=banks["de2", i, j][:], lhsT=dtc[k][:, P * j:P * (j + 1)].bitcast(E5M2), lhsT_scale=dts[k][:, P * j:P * (j + 1)],
+                                    rhs=w_c["fe", h][:].bitcast(E4M3), rhs_scale=w_s["fe", h][:], start=(h == 0), stop=(h == 1))
 
-        def de2_copy(eng_copy, i, j):
-            if j == 0:
+        def de2_copy(i, j):
+            if i not in outs:
                 outs[i] = st([P, 4, 512], F32, "o", "io8", 3)
-            eng_copy(out=outs[i][:, j, :], in_=mms[i, j][:])
+            copier("de2_copy", i, j)(out=outs[i][:, j, :], in_=banks["de2", i, j][:])
 
         def store(i, a, b):
             nc.sync.dma_start(out=o0v[i][:, a:b, :], in_=outs[i][:, a:b, :])
 
-        dws = {}
-        part = {}
+        def dw_pass(acc, k, m, start, stop):
+            i = k % GROUPS
+            nc.tensor.matmul_mx(out=acc[:], lhsT=ec[i][:, P * m:P * (m + 1)].bitcast(E4M3), lhsT_scale=es[i][:, P * m:P * (m + 1)],
+                                rhs=dzc[k][:].bitcast(E5M2), rhs_scale=dzs[k][:], start=start, stop=stop)
 
-        def dw(lo, hi, m, h):
-            dws[lo, m, h] = pt("mm", 3)
-            for i in range(lo, hi):
-                s = 2 * i + h
-                nc.tensor.matmul_mx(out=dws[lo, m, h][:], lhsT=ec[i][:, P * m:P * (m + 1)].bitcast(E4M3), lhsT_scale=es[i][:, P * m:P * (m + 1)],
-                                    rhs=dzc[s][:].bitcast(E5M2), rhs_scale=dzs[s][:], start=(i == lo), stop=(i == hi - 1))
+        def dw(k, m):
+            h, i = k // GROUPS, k % GROUPS
+            first = (0, PARKED)[h]
+            if i == first:
+                banks["dw", h, m] = pt("dw%d" % m, 1)
+            dw_pass(banks["dw", h, m], k, m, i == first, i == GROUPS - 1)
 
-        def dw_park(m, h):
-            if h == 0 and m % 2 == 0:
-                part[m] = st([P, 2, 1024], F32, "part", "z1t", 5)
-                part[m + 1] = part[m]
-            nc.scalar.copy(out=part[m][:, m % 2, 512 * h:512 * (h + 1)].rearrange("p (q t) -> p q t", t=4), in_=dws[0, m, h][:].rearrange("p (t q) -> p q t", t=4))
+        def dw_early(m):
+            banks["early", m] = pt("w", 3)
+            for i in range(PARKED):
+                dw_pass(banks["early", m], GROUPS + i, m, i == 0, i == PARKED - 1)
 
-        def dw_add(m, h):
-            dst = part[m][:, m % 2, 512 * h:512 * (h + 1)]
-            nc.vector.tensor_tensor(out=dst.rearrange("p (q t) -> p q t", t=4), in0=dws[SPLIT, m, h][:].rearrange("p (t q) -> p q t", t=4),
-                                    in1=dst.rearrange("p (q t) -> p q t", t=4), op=ALU.add)
-            nc.sync.dma_start(out=out_1[P * m:P * (m + 1), 512 * h:512 * (h + 1)], in_=dst)
+        def dw_park(m):
+            parts[m] = st([P, 512], F32, "part", "part", 4)
+            copier("dw_park", m)(out=parts[m][:].rearrange("p (q t) -> p q t", t=4), in_=banks["early", m][:].rearrange("p (t q) -> p q t", t=4))
 
-        vcopy = nc.vector.tensor_copy
-        scopy = nc.scalar.copy
+        def dw_out(h, m):
+            acc = banks["dw", h, m][:].rearrange("p (t q) -> p q t", t=4)
+            if h and PARKED:
+                dst = parts[m][:].rearrange("p (q t) -> p q t", t=4)
+                nc.vector.tensor_tensor(out=dst, in0=acc, in1=dst, op=ALU.add)
+            else:
+                parts[h, m] = st([P, 512], F32, "dwo", "dwo", 2)
+                copier("dw_out", h, m)(out=parts[h, m][:].rearrange("p (q t) -> p q t", t=4), in_=acc)
 
-        dz2_values(0, 1)
-        tp0 = dz2_turn(0)
-        dz2_copy(0, tp0)
-        tpa = wa_turn(0, 0)
-        tpb = wa_turn(0, 1)
-        dz2_quant(0, 1)
-        wa_copy(vcopy, 0, 0, tpa)
-        wa_copy(scopy, 0, 1, tpb)
-        wa_quant(0)
-        dagg(0)
-        mask(0)
-        for b in range(2):
-            wa_copy(scopy, 1, b, wa_turn(1, b))
+        def dw_store(h, m):
+            src = parts[m] if h and PARKED else parts[h, m]
+            nc.sync.dma_start(out=out_1[P * m:P * (m + 1), 512 * h:512 * (h + 1)], in_=src[:])
 
-        dw_jobs = [(m, h) for h in range(2) for m in range(4)]
-        for s in range(HALVES):
-            i, g = s // 2, s % 2
-            if s + 5 < HALVES:
-                load_z1(s + 5)
-            if g == 0 and 1 <= i < GROUPS - 1:
-                load_e2(i + 1)
-            done = (s - 3) // 2
-            if s >= 3:
-                for j in ((0, 1) if s % 2 == 1 else (2, 3)):
-                    de2(done, j)
-                    de2_copy(scopy, done, j)
-                if s % 2 == 0:
-                    store(done, 0, 4)
-            e2_copy(i, g)
-            if g == 0 and i > 0:
-                e2_quant(i - 1)
-            if s >= 10:
-                for m, h in dw_jobs[:2 if s % 3 == 1 else 1]:
-                    dw(0, SPLIT, m, h)
-                    dw_park(m, h)
-                dw_jobs = dw_jobs[2 if s % 3 == 1 else 1:]
-            product(s)
-            turn(s)
-            if s == 0:
-                wa_quant(1)
-                dagg(1)
-            if s + 1 < HALVES:
-                mask(s + 1)
-            if s > 0:
-                quant_feats(s - 1)
-            quant_edges(s)
-            untangle(scopy, s, 0)
-            untangle(scopy, s, 1)
-            if s == 0:
-                dz2_values(1, 4)
-            if s == 1:
-                for n in range(1, 4):
-                    dz2_copy(n, dz2_turn(n))
-                dz2_quant(1, 2)
-                dz2_quant(2, 4)
-                for b in range(2):
-                    fe_copy(scopy, 0, b, fe_turn(0, b))
-            if s == 2:
-                fe_quant(0)
-                for b in range(2):
-                    fe_copy(scopy, 1, b, fe_turn(1, b))
-            if s + 2 < HALVES:
-                dagg(s + 2)
-            if s == 2:
-                fe_quant(1)
-
-        e2_quant(7)
-        for j in (2, 3):
-            de2(6, j)
-            de2_copy(scopy, 6, j)
-        store(6, 0, 4)
-        quant_feats(15)
-        for m in range(4):
-            dw(SPLIT, GROUPS, m, 0)
-            dw_add(m, 0)
-        for j in range(4):
-            de2(7, j)
-            de2_copy(scopy, 7, j)
-            store(7, j, j + 1)
-        for m in range(4):
-            dw(SPLIT, GROUPS, m, 1)
-            dw_add(m, 1)
+        work = {"load_z1": load_z1, "load_e2": load_e2, "load_wa": load_wa, "load_fe": load_fe, "load_nodes": load_nodes, "dz2_values": dz2_values, "dz2_turn": dz2_turn,
+                "dz2_copy": dz2_copy, "dz2_quant": dz2_quant, "w_turn": w_turn, "w_copy": w_copy, "w_quant": w_quant, "dagg": dagg, "mask": mask, "product": product,
+                "quant_edges": quant_edges, "turn": turn, "untangle": untangle, "quant_feats": quant_feats, "e2_copy": e2_copy, "e2_quant": e2_quant, "de2": de2,
+                "de2_copy": de2_copy, "store": store, "dw": dw, "dw_early": dw_early, "dw_park": dw_park, "dw_out": dw_out, "dw_store": dw_store}
+        for job in ORDER:
+            work[job[0]](*job[1:])

from contextlib import ExitStack

import concourse.mybir as mybir
from concourse.masks import make_identity

F32 = mybir.dt.float32
BF16 = mybir.dt.bfloat16
U32 = mybir.dt.uint32
U8 = mybir.dt.uint8
E4M3 = mybir.dt.float8_e4m3fn_x4
E5M2 = mybir.dt.float8_e5m2_x4
ALU = mybir.AluOpType

FLOPS = 2 * 512 * 512 * 1024 + 2 * 2 * 4096 * 512 * 1024
BYTES = 2 * (4096 * 512 + 2 * 512 * 1024 + 512 * 512) + 4 * (4096 * 1024 + 512 * 512 + 4096 * 512 + 512 * 1024)

P = 128
GROUPS = 8
STEPS = 16
SLOPE = 0.2
PARKED = 5
SIGNED = (1, 2, 3, 4, 5, 6, 7, 8, 10, 12, 13, 14)
GE = (1, 2, 3, 4, 5, 6, 7)
DZC_BUFS = (3, 8)
DTC_BUFS = (4, 3)
ON_VECTOR = (
    ("w_copy", "wa", 0, 1),
    ("de2_copy", 0, 0),
    ("de2_copy", 0, 2),
    ("untangle", 2, 0),
    ("de2_copy", 0, 3),
    ("de2_copy", 1, 2),
    ("de2_copy", 2, 2),
    ("de2_copy", 2, 3),
    ("dw_park", 0),
    ("dw_park", 2),
    ("de2_copy", 3, 0),
    ("de2_copy", 3, 1),
    ("untangle", 13, 0),
    ("dw_out", 0, 1),
    ("dw_out", 0, 3),
    ("untangle", 7, 0),
    ("untangle", 15, 0),
    ("de2_copy", 7, 3),
    ("de2_copy", 7, 1),
    ("de2_copy", 7, 2),
)
ORDER = (
    ("load_nodes", 0, 1),
    ("load_nodes", 1, 4),
    ("load_wa", 0),
    ("load_z1", 0, 0, 1),
    ("load_e2", 0),
    ("load_wa", 1),
    ("load_z1", 0, 1, 2),
    ("load_z1", 1, 0, 2),
    ("load_fe",),
    ("dz2_values", 0, 1),
    ("dz2_turn", 0),
    ("dz2_copy", 0),
    ("dz2_quant", 0),
    ("load_z1", 2, 0, 2),
    ("dz2_values", 2, 4),
    ("w_turn", "wa", 0, 0),
    ("w_turn", "wa", 0, 1),
    ("dz2_values", 1, 2),
    ("w_copy", "wa", 0, 0),
    ("dz2_turn", 3),
    ("load_e2", 1),
    ("dz2_turn", 2),
    ("dz2_copy", 3),
    ("w_copy", "wa", 0, 1),
    ("dz2_copy", 2),
    ("dz2_turn", 1),
    ("dz2_quant", 3),
    ("w_quant", "wa", 0),
    ("dz2_copy", 1),
    ("mask", 0),
    ("dagg", 0),
    ("e2_copy", 0, 0),
    ("dz2_quant", 1),
    ("product", 0),
    ("w_turn", "wa", 1, 0),
    ("e2_copy", 0, 1),
    ("w_turn", "wa", 1, 1),
    ("w_copy", "wa", 1, 0),
    ("load_e2", 2),
    ("load_e2", 3),
    ("w_copy", "wa", 1, 1),
    ("e2_quant", 0),
    ("turn", 0, 0),
    ("mask", 8),
    ("w_quant", "wa", 1),
    ("turn", 0, 1),
    ("quant_edges", 0),
    ("dagg", 8),
    ("dz2_quant", 2),
    ("dw", 0, 1),
    ("dw", 0, 0),
    ("dw", 0, 3),
    ("dw", 0, 2),
    ("untangle", 0, 0),
    ("load_z1", 3, 0, 2),
    ("product", 8),
    ("untangle", 0, 1),
    ("mask", 1),
    ("quant_feats", 0),
    ("turn", 8, 1),
    ("mask", 9),
    ("turn", 8, 0),
    ("dagg", 1),
    ("quant_edges", 8),
    ("untangle", 8, 0),
    ("w_turn", "fe", 0, 0),
    ("load_z1", 4, 0, 2),
    ("product", 1),
    ("untangle", 8, 1),
    ("w_turn", "fe", 0, 1),
    ("w_copy", "fe", 0, 0),
    ("w_turn", "fe", 1, 0),
    ("quant_feats", 8),
    ("w_copy", "fe", 0, 1),
    ("w_turn", "fe", 1, 1),
    ("quant_edges", 1),
    ("w_copy", "fe", 1, 0),
    ("turn", 1, 0),
    ("w_quant", "fe", 0),
    ("w_copy", "fe", 1, 1),
    ("dagg", 9),
    ("untangle", 1, 0),
    ("turn", 1, 1),
    ("w_quant", "fe", 1),
    ("product", 9),
    ("de2", 0, 0),
    ("mask", 2),
    ("e2_copy", 1, 0),
    ("de2", 0, 2),
    ("de2_copy", 0, 0),
    ("e2_copy", 1, 1),
    ("dagg", 2),
    ("mask", 10),
    ("de2_copy", 0, 2),
    ("turn", 9, 1),
    ("product", 2),
    ("turn", 9, 0),
    ("load_e2", 4),
    ("untangle", 1, 1),
    ("load_z1", 5, 0, 2),
    ("e2_quant", 1),
    ("dagg", 10),
    ("quant_edges", 2),
    ("untangle", 9, 0),
    ("dw", 1, 3),
    ("dw", 1, 1),
    ("quant_feats", 1),
    ("turn", 2, 1),
    ("e2_copy", 2, 0),
    ("product", 10),
    ("untangle", 9, 1),
    ("de2", 0, 1),
    ("dw", 1, 2),
    ("mask", 3),
    ("turn", 2, 0),
    ("e2_copy", 2, 1),
    ("dw", 1, 0),
    ("untangle", 2, 0),
    ("dagg", 3),
    ("load_e2", 5),
    ("quant_feats", 9),
    ("turn", 10, 0),
    ("untangle", 2, 1),
    ("product", 3),
    ("untangle", 10, 0),
    ("de2", 1, 0),
    ("de2_copy", 0, 1),
    ("de2", 0, 3),
    ("mask", 11),
    ("de2_copy", 1, 0),
    ("turn", 3, 1),
    ("mask", 4),
    ("dagg", 11),
    ("quant_feats", 2),
    ("turn", 3, 0),
    ("load_z1", 6, 0, 2),
    ("e2_quant", 2),
    ("quant_edges", 3),
    ("dw", 2, 1),
    ("dw", 2, 3),
    ("de2_copy", 0, 3),
    ("e2_copy", 3, 0),
    ("untangle", 3, 0),
    ("dw", 2, 0),
    ("dw", 2, 2),
    ("product", 11),
    ("store", 0, 0, 4),
    ("turn", 10, 1),
    ("untangle", 3, 1),
    ("de2", 1, 2),
    ("e2_copy", 3, 1),
    ("untangle", 10, 1),
    ("de2", 1, 1),
    ("de2_copy", 1, 2),
    ("dagg", 4),
    ("load_e2", 6),
    ("quant_edges", 10),
    ("mask", 12),
    ("turn", 11, 1),
    ("e2_quant", 3),
    ("turn", 11, 0),
    ("quant_feats", 10),
    ("dw", 3, 2),
    ("dw", 3, 3),
    ("quant_feats", 3),
    ("dw", 3, 0),
    ("dw", 3, 1),
    ("quant_edges", 11),
    ("de2_copy", 1, 1),
    ("load_z1", 7, 0, 2),
    ("quant_edges", 9),
    ("untangle", 11, 0),
    ("de2", 2, 0),
    ("e2_copy", 4, 0),
    ("product", 4),
    ("de2_copy", 2, 0),
    ("de2", 1, 3),
    ("untangle", 11, 1),
    ("de2", 2, 2),
    ("e2_copy", 4, 1),
    ("de2_copy", 2, 2),
    ("de2_copy", 1, 3),
    ("dagg", 12),
    ("turn", 4, 0),
    ("mask", 5),
    ("product", 12),
    ("store", 1, 0, 4),
    ("load_e2", 7),
    ("de2", 2, 3),
    ("turn", 4, 1),
    ("e2_quant", 4),
    ("untangle", 4, 0),
    ("dagg", 5),
    ("quant_edges", 12),
    ("quant_edges", 4),
    ("untangle", 4, 1),
    ("dw_early", 1),
    ("quant_feats", 11),
    ("mask", 13),
    ("e2_copy", 5, 0),
    ("product", 5),
    ("dw", 4, 0),
    ("dw_early", 0),
    ("e2_copy", 5, 1),
    ("de2_copy", 2, 3),
    ("dw", 4, 2),
    ("dw_park", 1),
    ("dagg", 13),
    ("dw_park", 0),
    ("dw", 4, 3),
    ("mask", 6),
    ("turn", 5, 1),
    ("product", 13),
    ("turn", 5, 0),
    ("dw_early", 2),
    ("untangle", 5, 0),
    ("e2_quant", 5),
    ("dagg", 6),
    ("quant_edges", 5),
    ("dw", 4, 1),
    ("untangle", 5, 1),
    ("de2", 3, 0),
    ("quant_feats", 4),
    ("dw", 5, 1),
    ("dw_park", 2),
    ("e2_copy", 6, 0),
    ("dw", 5, 0),
    ("mask", 14),
    ("turn", 12, 1),
    ("de2_copy", 3, 0),
    ("product", 6),
    ("turn", 12, 0),
    ("e2_copy", 6, 1),
    ("dw_early", 3),
    ("untangle", 12, 0),
    ("dw", 5, 2),
    ("quant_feats", 5),
    ("dw", 5, 3),
    ("untangle", 12, 1),
    ("quant_edges", 6),
    ("de2", 3, 2),
    ("e2_quant", 6),
    ("dagg", 14),
    ("dw_park", 3),
    ("de2", 3, 3),
    ("product", 14),
    ("e2_copy", 7, 0),
    ("de2_copy", 3, 2),
    ("turn", 13, 1),
    ("de2_copy", 3, 3),
    ("dw", 6, 1),
    ("mask", 7),
    ("de2", 3, 1),
    ("e2_copy", 7, 1),
    ("turn", 13, 0),
    ("de2_copy", 3, 1),
    ("dw", 6, 0),
    ("untangle", 13, 0),
    ("store", 3, 0, 4),
    ("dagg", 7),
    ("de2", 2, 1),
    ("untangle", 13, 1),
    ("dw", 6, 2),
    ("quant_feats", 12),
    ("turn", 6, 0),
    ("quant_edges", 13),
    ("de2_copy", 2, 1),
    ("de2", 4, 0),
    ("quant_feats", 13),
    ("untangle", 6, 0),
    ("store", 2, 0, 4),
    ("de2", 4, 2),
    ("product", 7),
    ("dw", 6, 3),
    ("de2_copy", 4, 0),
    ("de2", 4, 3),
    ("de2_copy", 4, 2),
    ("de2", 4, 1),
    ("de2_copy", 4, 3),
    ("turn", 6, 1),
    ("e2_quant", 7),
    ("de2_copy", 4, 1),
    ("turn", 14, 0),
    ("quant_edges", 7),
    ("untangle", 6, 1),
    ("store", 4, 0, 4),
    ("turn", 14, 1),
    ("mask", 15),
    ("dw", 7, 3),
    ("untangle", 14, 0),
    ("dw", 7, 1),
    ("de2", 5, 0),
    ("dw_out", 0, 1),
    ("dw", 7, 0),
    ("untangle", 14, 1),
    ("quant_edges", 14),
    ("dw", 7, 2),
    ("dw_store", 0, 1),
    ("dagg", 15),
    ("quant_feats", 6),
    ("de2", 5, 3),
    ("dw_out", 0, 2),
    ("dw", 13, 1),
    ("quant_feats", 14),
    ("dw", 14, 1),
    ("de2_copy", 5, 0),
    ("dw_store", 0, 2),
    ("de2", 5, 2),
    ("product", 15),
    ("de2_copy", 5, 3),
    ("de2", 5, 1),
    ("de2_copy", 5, 2),
    ("de2", 6, 0),
    ("de2_copy", 5, 1),
    ("de2", 6, 1),
    ("de2_copy", 6, 0),
    ("dw_out", 0, 3),
    ("store", 5, 0, 4),
    ("de2", 6, 2),
    ("de2_copy", 6, 1),
    ("quant_edges", 15),
    ("turn", 7, 0),
    ("dw_store", 0, 3),
    ("de2_copy", 6, 2),
    ("turn", 7, 1),
    ("dw_out", 0, 0),
    ("untangle", 7, 0),
    ("dw", 15, 1),
    ("untangle", 7, 1),
    ("de2", 6, 3),
    ("dw_store", 0, 0),
    ("dw_out", 1, 1),
    ("dw", 13, 2),
    ("turn", 15, 0),
    ("de2_copy", 6, 3),
    ("dw_store", 1, 1),
    ("quant_feats", 7),
    ("turn", 15, 1),
    ("store", 6, 0, 4),
    ("untangle", 15, 0),
    ("dw", 14, 2),
    ("untangle", 15, 1),
    ("dw", 15, 2),
    ("dw", 13, 0),
    ("dw", 13, 3),
    ("dw_out", 1, 2),
    ("dw", 14, 3),
    ("dw", 15, 3),
    ("quant_feats", 15),
    ("dw_store", 1, 2),
    ("dw", 14, 0),
    ("dw", 15, 0),
    ("dw_out", 1, 3),
    ("de2", 7, 0),
    ("dw_out", 1, 0),
    ("dw_store", 1, 3),
    ("de2", 7, 3),
    ("de2_copy", 7, 0),
    ("dw_store", 1, 0),
    ("de2", 7, 1),
    ("de2_copy", 7, 3),
    ("store", 7, 0, 1),
    ("de2", 7, 2),
    ("de2_copy", 7, 1),
    ("store", 7, 3, 4),
    ("de2_copy", 7, 2),
    ("store", 7, 1, 2),
    ("store", 7, 2, 3),
)


def tile_graph_gan_pb_v_kernel(tc, e2, x, fe_w2, fe_b2, fn_w0, fn_b0, z1, z2, grad_out, out_0, out_1):
    nc = tc.nc
    with ExitStack() as ctx:
        sb = ctx.enter_context(tc.tile_pool(name="sb", bufs=1))
        ps = ctx.enter_context(tc.psum_pool(name="ps", bufs=1))
        ctx.enter_context(tc.manual_schedule())

        def st(shape, dtype, name, tag, bufs):
            return sb.tile(shape, dtype, name=name, tag=tag, bufs=bufs, align_bytes=64)

        def pt(tag, bufs):
            t = ps.tile([P, 512], F32, name=tag, tag=tag, bufs=bufs)
            return t

        def copier(*job):
            return nc.vector.tensor_copy if job in ON_VECTOR else nc.scalar.copy

        z1v = z1.flatten_outer_dims().rearrange("(i p j) w -> i p j w", p=P, j=4)
        e2v = e2.flatten_outer_dims().rearrange("(i p j) f -> i p j f", p=P, j=4)
        o0v = out_0.flatten_outer_dims().rearrange("(i p j) f -> i p j f", p=P, j=4)
        wav = fn_w0[0:1024, :].rearrange("(g m t) k -> g m t k", g=2, t=4)
        fev = fe_w2.rearrange("(r p) k -> p r k", p=P)
        z2v = z2.flatten_outer_dims().rearrange("(n p) k -> p n k", p=P)
        gov = grad_out.flatten_outer_dims().rearrange("(n p) k -> p n k", p=P)

        ident = st([P, P], F32, "ident", "ident", 1)
        make_identity(nc, ident[:])

        z1t = {}
        e2t = {}
        wa_raw = {}
        z2t = st([P, 4, 512], F32, "z2t", "io8", 3)
        got = st([P, 4, 512], BF16, "got", "n4", 2)
        dz2 = st([P, 4, 512], BF16, "dz2", "n4", 2)
        fe_raw = {}

        def load_z1(i, a, b):
            if i not in z1t:
                z1t[i] = st([P, 4096], F32, "z1t", "z1t", 3)
            if i == 0:
                dst = z1t[i][:, 2048 * a:2048 * b].rearrange("p (j w) -> p j w", j=4)
            else:
                dst = z1t[i][:].rearrange("p (j w) -> p j w", j=4)
            nc.sync.dma_start(out=dst, in_=z1v[i][:, :, 512 * a:512 * b])

        def load_e2(i):
            e2t[i] = st([P, 4, 512], BF16, "e2t", "k4", 3)
            nc.sync.dma_start(out=e2t[i][:], in_=e2v[i])

        def load_wa(h):
            wa_raw[h] = st([P, 4, 512], BF16, "wa_raw", "k4", 3)
            nc.sync.dma_start(out=wa_raw[h][:], in_=wav[h])

        def load_fe():
            fe_raw[0] = st([P, 4, 1024], BF16, "fe_raw", "io8", 3)
            nc.sync.dma_start(out=fe_raw[0][:], in_=fev)

        def load_nodes(a, b):
            nc.sync.dma_start(out=z2t[:, a:b, :], in_=z2v[:, a:b, :])
            nc.sync.dma_start(out=got[:, a:b, :], in_=gov[:, a:b, :])

        banks = {}
        dz2_t = {}
        dz2_c = {}
        dz2_s = {}

        def dz2_values(a, b):
            nc.vector.tensor_scalar(out=z2t[:, a:b, :], in0=z2t[:, a:b, :], scalar1=0.0, scalar2=SLOPE, op0=ALU.is_gt, op1=ALU.max)
            nc.vector.tensor_tensor(out=dz2[:, a:b, :], in0=got[:, a:b, :], in1=z2t[:, a:b, :], op=ALU.mult)

        def dz2_turn(n):
            banks["dz2", n] = pt("w", 3)
            words = dz2[:, n, :].bitcast(F32)
            for u in range(2):
                nc.tensor.transpose(banks["dz2", n][:, P * u:P * (u + 1)], words[:, u:256:2], ident[:])

        def dz2_copy(n):
            dz2_t[n] = st([P, 1024], BF16, "dz2_t", "dz2_t", 2)
            dst = dz2_t[n][:].bitcast(F32).rearrange("p (n d u) -> p n d u", d=2, u=2)
            src = banks["dz2", n][:, 0:256].rearrange("p (u n) -> p n u", u=2).unsqueeze(2).to_broadcast([P, P, 2, 2])
            copier("dz2_copy", n)(out=dst, in_=src)

        def dz2_quant(n):
            dz2_c[n] = st([P, 256], U32, "dz2_c", "dz2_c", 4)
            dz2_s[n] = st([P, 256], U8, "dz2_s", "dz2_s", 4)
            nc.vector.quantize_mx(out=dz2_c[n][:].bitcast(E5M2), scales=dz2_s[n][:], in_=dz2_t[n][:])

        w_g = {}
        w_c = {}
        w_s = {}

        def w_turn(w, h, b):
            banks[w, h, b] = pt("w", 3)
            for s in range(2):
                for u in range(2):
                    r = 2 * b + s
                    if w == "wa":
                        words = wa_raw[h][:, r, :].bitcast(F32)[:, u:256:2]
                    else:
                        words = fe_raw[0][:, r, :].bitcast(F32)[:, 256 * h + u:256 * (h + 1):2]
                    nc.tensor.transpose(banks[w, h, b][:, P * (2 * s + u):P * (2 * s + u + 1)], words, ident[:])

        def w_copy(w, h, b):
            if (w, h) not in w_g:
                w_g[w, h] = st([P, 2048], BF16, "w_g", "w_g", 2)
            words = w_g[w, h][:].bitcast(F32)[:, 512 * b:512 * (b + 1)]
            copier("w_copy", w, h, b)(out=words.rearrange("p (s m u) -> p s m u", s=2, u=2), in_=banks[w, h, b][:].rearrange("p (s u m) -> p s m u", s=2, u=2))

        def w_quant(w, h):
            w_c[w, h] = st([P, 512], U32, "w_c", "w_c", 4)
            w_s[w, h] = st([P, 512], U8, "w_s", "w_s", 4)
            nc.vector.quantize_mx(out=w_c[w, h][:].bitcast(E4M3), scales=w_s[w, h][:], in_=w_g[w, h][:])

        d_ps = {}
        mk = {}
        dz = {}
        dzc = {}
        dzs = {}
        dzt = {}
        dtc = {}
        dts = {}

        def dagg(k):
            h, i = k // GROUPS, k % GROUPS
            d_ps[k] = pt("d", 1)
            cols = slice(P * (i % 2), P * (i % 2 + 1))
            nc.tensor.matmul_mx(out=d_ps[k][:], lhsT=dz2_c[i // 2][:, cols].bitcast(E5M2), lhsT_scale=dz2_s[i // 2][:, cols],
                                rhs=w_c["wa", h][:].bitcast(E4M3), rhs_scale=w_s["wa", h][:], start=True, stop=True)

        def mask(k):
            mk[k] = st([P, 2048], F32, "mk", "mk", 2)
            out = mk[k][:].rearrange("p (t q j) -> p q j t", t=4, j=4)
            h, i = k // GROUPS, k % GROUPS
            if i == 0:
                z = z1t[i][:, 2048 * h:2048 * (h + 1)].rearrange("p (j q t) -> p q j t", j=4, t=4)
            else:
                z = z1t[i][:].rearrange("p (j h q t) -> p h q j t", j=4, h=2, t=4)[:, h]
            if k in SIGNED:
                nc.scalar.activation(out=out, in_=z, func=mybir.ActivationFunctionType.Sign)
            else:
                nc.vector.tensor_scalar(out=out, in0=z, scalar1=0.0, scalar2=SLOPE, op0=ALU.is_gt, op1=ALU.max)

        def product(k):
            dz[k] = st([P, 2048], BF16, "dz", "dz", 3)
            out = dz[k][:].rearrange("p (c j) -> p c j", j=4)
            slope = mk[k][:].rearrange("p (c j) -> p c j", j=4)
            grad = d_ps[k][:].unsqueeze(2).to_broadcast([P, 512, 4])
            if k in SIGNED:
                nc.vector.scalar_tensor_tensor(out=out, in0=slope, scalar=SLOPE, in1=grad, op0=ALU.max, op1=ALU.mult)
            else:
                nc.vector.tensor_tensor(out=out, in0=slope, in1=grad, op=ALU.mult)

        def quant_edges(k):
            h = k // GROUPS
            dzc[k] = st([P, 512], U32, "dzc", "dzc%d" % h, DZC_BUFS[h])
            dzs[k] = st([P, 512], U8, "dzs", "dzs%d" % h, DZC_BUFS[h])
            nc.vector.quantize_mx(out=dzc[k][:].bitcast(E5M2), scales=dzs[k][:], in_=dz[k][:])

        def turn(k, u):
            words = dz[k][:].bitcast(F32)
            banks["dz", k, u] = pt("w", 3)
            for t in range(4):
                nc.tensor.transpose(banks["dz", k, u][:, P * t:P * (t + 1)], words[:, 256 * t + u:256 * (t + 1):2], ident[:])

        def untangle(k, u):
            if k not in dzt:
                dzt[k] = st([P, 2048], BF16, "dzt", "dzt", 2)
            copier("untangle", k, u)(out=dzt[k][:, 1024 * u:1024 * (u + 1)].rearrange("p (e n t) -> p e n t", e=2, t=4),
                                     in_=banks["dz", k, u][:].bitcast(BF16).rearrange("p (t n e) -> p e n t", t=4, e=2))

        def quant_feats(k):
            h = k // GROUPS
            dtc[k] = st([P, 512], U32, "dtc", "dtc%d" % h, DTC_BUFS[h])
            dts[k] = st([P, 512], U8, "dts", "dts%d" % h, DTC_BUFS[h])
            nc.vector.quantize_mx(out=dtc[k][:].bitcast(E5M2), scales=dts[k][:], in_=dzt[k][:])

        eg = {}
        ec = {}
        es = {}

        def e2_copy(i, b):
            if i not in eg:
                eg[i] = st([P, 2048], BF16, "eg", "eg", 1)
            lo = 256 * b
            dst = eg[i][:, 4 * lo:4 * lo + 1024]
            if i in GE:
                for c in (0, 128):
                    nc.gpsimd.tensor_scalar(out=dst[:, 4 * c:4 * c + 512].rearrange("p (c j) -> p c j", j=4), in0=e2t[i][:, :, lo + c:lo + c + 128].rearrange("p j c -> p c j"),
                                            scalar1=1.0, scalar2=0.0, op0=ALU.mult, op1=ALU.add)
            else:
                nc.scalar.copy(out=dst.rearrange("p (c i j) -> p c j i", i=4, j=4), in_=e2t[i][:, :, lo:lo + 256].rearrange("p j (c i) -> p c j i", i=4))

        def e2_quant(i):
            ec[i] = st([P, 512], U32, "ec", "ec", GROUPS)
            es[i] = st([P, 512], U8, "es", "es", GROUPS)
            nc.vector.quantize_mx(out=ec[i][:].bitcast(E4M3), scales=es[i][:], in_=eg[i][:])

        outs = {}
        parts = {}

        def de2(i, j):
            banks["de2", i, j] = pt("w", 3)
            for h in range(2):
                k = GROUPS * h + i
                nc.tensor.matmul_mx(out=banks["de2", i, j][:], lhsT=dtc[k][:, P * j:P * (j + 1)].bitcast(E5M2), lhsT_scale=dts[k][:, P * j:P * (j + 1)],
                                    rhs=w_c["fe", h][:].bitcast(E4M3), rhs_scale=w_s["fe", h][:], start=(h == 0), stop=(h == 1))

        def de2_copy(i, j):
            if i not in outs:
                outs[i] = st([P, 4, 512], F32, "o", "io8", 3)
            copier("de2_copy", i, j)(out=outs[i][:, j, :], in_=banks["de2", i, j][:])

        def store(i, a, b):
            nc.sync.dma_start(out=o0v[i][:, a:b, :], in_=outs[i][:, a:b, :])

        def dw_pass(acc, k, m, start, stop):
            i = k % GROUPS
            nc.tensor.matmul_mx(out=acc[:], lhsT=ec[i][:, P * m:P * (m + 1)].bitcast(E4M3), lhsT_scale=es[i][:, P * m:P * (m + 1)],
                                rhs=dzc[k][:].bitcast(E5M2), rhs_scale=dzs[k][:], start=start, stop=stop)

        def dw(k, m):
            h, i = k // GROUPS, k % GROUPS
            first = (0, PARKED)[h]
            if i == first:
                banks["dw", h, m] = pt("dw%d" % m, 1)
            dw_pass(banks["dw", h, m], k, m, i == first, i == GROUPS - 1)

        def dw_early(m):
            banks["early", m] = pt("w", 3)
            for i in range(PARKED):
                dw_pass(banks["early", m], GROUPS + i, m, i == 0, i == PARKED - 1)

        def dw_park(m):
            parts[m] = st([P, 512], F32, "part", "part", 4)
            copier("dw_park", m)(out=parts[m][:].rearrange("p (q t) -> p q t", t=4), in_=banks["early", m][:].rearrange("p (t q) -> p q t", t=4))

        def dw_out(h, m):
            acc = banks["dw", h, m][:].rearrange("p (t q) -> p q t", t=4)
            if h and PARKED:
                dst = parts[m][:].rearrange("p (q t) -> p q t", t=4)
                nc.vector.tensor_tensor(out=dst, in0=acc, in1=dst, op=ALU.add)
            else:
                parts[h, m] = st([P, 512], F32, "dwo", "dwo", 2)
                copier("dw_out", h, m)(out=parts[h, m][:].rearrange("p (q t) -> p q t", t=4), in_=acc)

        def dw_store(h, m):
            src = parts[m] if h and PARKED else parts[h, m]
            nc.sync.dma_start(out=out_1[P * m:P * (m + 1), 512 * h:512 * (h + 1)], in_=src[:])

        work = {"load_z1": load_z1, "load_e2": load_e2, "load_wa": load_wa, "load_fe": load_fe, "load_nodes": load_nodes, "dz2_values": dz2_values, "dz2_turn": dz2_turn,
                "dz2_copy": dz2_copy, "dz2_quant": dz2_quant, "w_turn": w_turn, "w_copy": w_copy, "w_quant": w_quant, "dagg": dagg, "mask": mask, "product": product,
                "quant_edges": quant_edges, "turn": turn, "untangle": untangle, "quant_feats": quant_feats, "e2_copy": e2_copy, "e2_quant": e2_quant, "de2": de2,
                "de2_copy": de2_copy, "store": store, "dw": dw, "dw_early": dw_early, "dw_park": dw_park, "dw_out": dw_out, "dw_store": dw_store}
        for job in ORDER:
            work[job[0]](*job[1:])
